import numpy as np
import ml_dtypes


def mxq(x, axis, fmt="e4m3"):
    dtype, down = {"e4m3": (ml_dtypes.float8_e4m3fn, 7), "e5m2": (ml_dtypes.float8_e5m2, 14)}[fmt]
    v = np.moveaxis(np.asarray(x, np.float32).astype(ml_dtypes.bfloat16).astype(np.float64), axis, -1)
    blocks = v.reshape(v.shape[:-1] + (-1, 32))
    amax = np.abs(blocks).max(-1, keepdims=True)
    byte = np.maximum(np.where(amax > 0, np.frexp(amax)[1] - 1 + 127, 0) - down, 1)
    scale = np.exp2(byte - 127.0)
    codes = (blocks / scale).astype(np.float32).astype(dtype).astype(np.float64)
    return np.moveaxis((codes * scale).reshape(v.shape), -1, axis)


WIDE = False


def mx_kscale(k):
    if not WIDE:
        return np.ones(k)
    levels = np.array([10, -10, 5, -5, 0])
    a = np.random.permutation(np.resize(levels, k // 512 * 4)).reshape(k // 512, 4)
    idx = np.arange(k)
    return np.exp2(a[idx // 512, idx % 128 // 32])


BF16 = ml_dtypes.bfloat16


def bf(x):
    return np.asarray(x, np.float32).astype(BF16)


def f64(x):
    return np.asarray(x).astype(np.float64)


E2M1 = np.array([0.0, 0.5, 1.0, 1.5, 2.0, 3.0, 4.0, 6.0, -0.0, -0.5, -1.0, -1.5, -2.0, -3.0, -4.0, -6.0])


def pack_weight(w, fmt):
    k, n = w.shape
    w = f64(bf(w)).reshape(k // 32, 32, n)
    amax = np.abs(w).max(1)
    if fmt == "e4m3":
        byte = np.frexp(amax)[1] - 1 + 127 - 7
    else:
        mant, ex = np.frexp(amax / 6.0)
        byte = np.where(mant > 0.5, ex, ex - 1) + 127
    byte = np.clip(np.where(amax > 0, byte, 1), 1, 254)
    scaled = (w * np.exp2(127.0 - byte)[:, None, :]).reshape(k, n).astype(np.float32)
    by_word = np.ascontiguousarray(scaled.reshape(k // 512, 128, 4, n).transpose(0, 1, 3, 2))
    if fmt == "e4m3":
        words = by_word.astype(ml_dtypes.float8_e4m3fn).view(np.uint8)
    else:
        c = by_word.astype(ml_dtypes.float4_e2m1fn).view(np.uint8) & 0xF
        words = c[..., 0::2] | (c[..., 1::2] << 4)
    return np.ascontiguousarray(words), np.ascontiguousarray(byte.astype(np.uint8).reshape(k // 512, 16, n))


def unpack_weight(words, scales, fmt):
    g, p, n, _ = words.shape
    if fmt == "e4m3":
        vals = np.ascontiguousarray(words).view(ml_dtypes.float8_e4m3fn).astype(np.float64)
    else:
        nib = np.empty((g, p, n, 4), np.uint8)
        nib[..., 0::2] = words & 0xF
        nib[..., 1::2] = words >> 4
        vals = E2M1[nib]
    vals = vals * np.repeat(np.exp2(scales.astype(np.float64) - 127.0), 8, axis=1)[..., None]
    return vals.transpose(0, 1, 3, 2).reshape(g * 512, n)


B, D, R = 8192, 1024, 128
FMT = "e4m3"


def softplus(v):
    return np.log1p(np.exp(v))


def setup_inputs():
    s = mx_kscale(D)
    w = 1.0 / np.sqrt(D)
    x = bf(np.random.standard_normal((B, D)) * s)
    state_re = bf(np.random.standard_normal((B, R)))
    state_im = bf(np.random.standard_normal((B, R)))
    W_dt_words, W_dt_scales = pack_weight((np.random.standard_normal((R, D)) * 0.5 * w / s).T, FMT)
    b_dt = bf(np.random.standard_normal(R) * 0.3)
    W_ph_words, W_ph_scales = pack_weight((np.random.standard_normal((R, D)) * 0.5 * w / s).T, FMT)
    b_ph = bf(np.random.standard_normal(R) * 0.3)
    W_B_words, W_B_scales = pack_weight((np.random.standard_normal((R, D)) * w / s).T, FMT)
    A_real = bf(np.random.standard_normal(R) * 0.5)
    A_imag = bf(np.random.standard_normal(R) * 0.5)
    return {"x": x,
            "state_re": state_re,
            "state_im": state_im,
            "W_dt_words": W_dt_words,
            "W_dt_scales": W_dt_scales,
            "b_dt": b_dt,
            "W_ph_words": W_ph_words,
            "W_ph_scales": W_ph_scales,
            "b_ph": b_ph,
            "W_B_words": W_B_words,
            "W_B_scales": W_B_scales,
            "A_real": A_real,
            "A_imag": A_imag}


def reference(x, state_re, state_im, W_dt_words, W_dt_scales, b_dt, W_ph_words, W_ph_scales, b_ph, W_B_words, W_B_scales, A_real, A_imag):
    xq = mxq(f64(x), 1, "e4m3")
    dt = softplus((xq @ unpack_weight(W_dt_words, W_dt_scales, FMT)) + f64(b_dt))
    phase = np.tanh((xq @ unpack_weight(W_ph_words, W_ph_scales, FMT)) + f64(b_ph)) * np.pi
    decay = np.exp(-dt * np.exp(f64(A_real)))
    angle = dt * f64(A_imag) + phase
    B_val = xq @ unpack_weight(W_B_words, W_B_scales, FMT)
    cos = np.cos(angle)
    sin = np.sin(angle)
    new_re = (f64(state_re) * cos - f64(state_im) * sin) * decay + B_val
    new_im = (f64(state_re) * sin + f64(state_im) * cos) * decay
    return new_re, new_im

@@ -1,0 +1,285 @@
+import math
+from contextlib import ExitStack
+
+import concourse.mybir as mybir
+from concourse.masks import make_identity
+
+F32 = mybir.dt.float32
+BF16 = mybir.dt.bfloat16
+I32 = mybir.dt.int32
+U32 = mybir.dt.uint32
+U8 = mybir.dt.uint8
+FP8X4 = mybir.dt.float8_e4m3fn_x4
+ACT = mybir.ActivationFunctionType
+ALU = mybir.AluOpType
+
+P = 128
+ROWS = 8192
+D_MODEL = 1024
+PASSES = 2
+BLOCKS = 4
+CHUNK = BLOCKS * P
+N_CHUNKS = ROWS // CHUNK
+ROWS_PER_PARTITION = ROWS // P
+ROUND_CHUNKS = 4
+ROUND = ROUND_CHUNKS * CHUNK
+HALF = ROUND // 2
+N_WEIGHTS = 3
+W_DT, W_PH, W_B = 0, 1, 2
+LOADS_AHEAD = 2
+ROTATE_LAG = 3
+ROUND_TO_INT = 1.5 * 2.0**23
+TWO_PI = 2.0 * math.pi
+
+FLOPS = 2 * ROWS * D_MODEL * N_WEIGHTS * P
+
+
+def tile_mamba3mimoblock_pa_t_kernel(
+    tc,
+    x,
+    state_re,
+    state_im,
+    W_dt_words,
+    W_dt_scales,
+    b_dt,
+    W_ph_words,
+    W_ph_scales,
+    b_ph,
+    W_B_words,
+    W_B_scales,
+    A_real,
+    A_imag,
+    out_0,
+    out_1,
+):
+    nc = tc.nc
+    x_rows = x.rearrange("(p i) k -> p i k", i=ROWS_PER_PARTITION)
+    re_rows = state_re.rearrange("(p i) n -> p (i n)", i=ROWS_PER_PARTITION)
+    im_rows = state_im.rearrange("(p i) n -> p (i n)", i=ROWS_PER_PARTITION)
+    new_re_rows = out_0.rearrange("(p i) n -> p (i n)", i=ROWS_PER_PARTITION)
+    new_im_rows = out_1.rearrange("(p i) n -> p (i n)", i=ROWS_PER_PARTITION)
+
+    with ExitStack() as stack:
+        consts = stack.enter_context(tc.tile_pool(name="consts", bufs=1))
+        sbuf = stack.enter_context(tc.tile_pool(name="sbuf", bufs=2))
+        psum = stack.enter_context(tc.psum_pool(name="psum", bufs=1))
+        stack.enter_context(tc.manual_schedule())
+
+        x_tiles, grouped, codes, scales = {}, {}, {}, {}
+        state, neg_dt, turns, decay, sin_d, cos_d = {}, {}, {}, {}, {}, {}
+
+        def load_x(c):
+            x_tiles[c] = sbuf.tile([P, BLOCKS, D_MODEL], BF16, name="x_sb", tag="x_sb", bufs=LOADS_AHEAD + 1)
+            nc.sync.dma_start(out=x_tiles[c][:], in_=x_rows[:, BLOCKS * c : BLOCKS * (c + 1), :])
+
+        load_x(0)
+
+        w_scales = consts.tile([P, N_WEIGHTS, PASSES, P], U8, align_bytes=64)
+        nc.vector.memset(w_scales[:].rearrange("p w g n -> p (w g n)").bitcast(I32), 0)
+        w_words = consts.tile([P, N_WEIGHTS, PASSES, P], U32, align_bytes=64)
+
+        def load_weight(w, words, scale_rows):
+            for quadrant in range(4):
+                nc.sync.dma_start(
+                    out=w_scales[32 * quadrant : 32 * quadrant + 4, w, :, :].bitcast(I32),
+                    in_=scale_rows[:, 4 * quadrant : 4 * quadrant + 4, :].rearrange("g q n -> q g n").bitcast(I32),
+                )
+            nc.sync.dma_start(
+                out=w_words[:, w, :, :].bitcast(I32),
+                in_=words.rearrange("g p n t -> p g (n t)").bitcast(I32),
+            )
+
+        load_weight(W_DT, W_dt_words, W_dt_scales)
+        load_weight(W_PH, W_ph_words, W_ph_scales)
+        load_x(1)
+        load_weight(W_B, W_B_words, W_B_scales)
+
+        identity = consts.tile([P, P], F32)
+        make_identity(nc, identity[:])
+        identity_bf = consts.tile([P, P], BF16)
+        make_identity(nc, identity_bf[:])
+
+        vector_rows = consts.tile([P, P], BF16)
+        nc.vector.memset(vector_rows[:].bitcast(I32), 0)
+        for j, vector in enumerate((b_dt, b_ph, A_real, A_imag)):
+            nc.scalar.dma_start(out=vector_rows[j : j + 1, :], in_=vector.unsqueeze(0))
+        vector_cols = psum.tile([P, P], BF16, tag="cos_t")
+        nc.tensor.transpose(vector_cols[:], vector_rows[:], identity_bf[:])
+        per_channel = consts.tile([P, 4], F32)
+        nc.vector.tensor_copy(out=per_channel[:], in_=vector_cols[:, 0:4])
+
+        neg_b_dt = consts.tile([P, 1], F32)
+        nc.vector.tensor_scalar_mul(out=neg_b_dt[:], in0=per_channel[:, 0:1], scalar1=-1.0)
+        two_b_ph = consts.tile([P, 1], F32)
+        nc.vector.tensor_scalar_mul(out=two_b_ph[:], in0=per_channel[:, 1:2], scalar1=2.0)
+        decay_rate = consts.tile([P, 1], F32)
+        nc.scalar.activation(out=decay_rate[:], in_=per_channel[:, 2:3], func=ACT.Exp)
+        neg_turn_rate = consts.tile([P, 1], F32)
+        nc.vector.tensor_scalar_mul(out=neg_turn_rate[:], in0=per_channel[:, 3:4], scalar1=-1.0 / TWO_PI)
+
+        def transpose_chunk(c):
+            grouped[c] = sbuf.tile([P, PASSES, 4 * CHUNK], BF16, name="grouped", tag="grouped", align_bytes=64)
+            for g in range(PASSES):
+                pairs = grouped[c][:, g, :].bitcast(F32).rearrange("p (row u) -> p row u", u=2)
+                for h in range(BLOCKS // 2):
+                    xt = psum.tile([P, 2, 2 * P], F32, tag="xt", bufs=3)
+                    for u in range(2):
+                        for b in range(2):
+                            x_words = x_tiles[c][:, 2 * h + b, :].bitcast(F32)
+                            nc.tensor.transpose(
+                                xt[:, u, P * b : P * (b + 1)],
+                                x_words[:, 256 * g + u : 256 * (g + 1) : 2],
+                                identity[:],
+                            )
+                    rows_out = pairs[:, 2 * P * h : 2 * P * (h + 1), :]
+                    if h % 2 == 0:
+                        nc.scalar.copy(out=rows_out, in_=xt[:].rearrange("p u row -> p row u"))
+                    else:
+                        nc.vector.tensor_copy(out=rows_out, in_=xt[:].rearrange("p u row -> p row u"))
+
+        def quantise_chunk(c):
+            codes[c] = sbuf.tile([P, PASSES * CHUNK], U32, name="codes", tag="codes", bufs=8, align_bytes=64)
+            scales[c] = sbuf.tile([P, PASSES * CHUNK], U8, name="scales", tag="scales", bufs=8, align_bytes=64)
+            nc.vector.quantize_mx(
+                out=codes[c][:].bitcast(FP8X4),
+                scales=scales[c][:],
+                in_=grouped[c][:].rearrange("p g n -> p (g n)"),
+            )
+
+        def project(c, w, tag):
+            acc = psum.tile([P, CHUNK], F32, name=tag, tag=tag)
+            for g in range(PASSES):
+                k_cols = slice(g * CHUNK, (g + 1) * CHUNK)
+                nc.tensor.matmul_mx(
+                    out=acc[:],
+                    lhsT=w_words[:, w, g, :].bitcast(FP8X4),
+                    lhsT_scale=w_scales[:, w, g, :],
+                    rhs=codes[c][:, k_cols].bitcast(FP8X4),
+                    rhs_scale=scales[c][:, k_cols],
+                    start=(g == 0),
+                    stop=(g == PASSES - 1),
+                )
+            return acc
+
+        def gates(r):
+            state[r] = sbuf.tile([P, 2, ROUND], BF16, name="state", tag="state")
+            nc.sync.dma_start(out=state[r][:, 0, :], in_=re_rows[:, r * ROUND : (r + 1) * ROUND])
+            nc.sync.dma_start(out=state[r][:, 1, :], in_=im_rows[:, r * ROUND : (r + 1) * ROUND])
+            neg_dt[r] = sbuf.tile([P, ROUND], F32, name="neg_dt", tag="neg_dt", bufs=1)
+            turns[r] = sbuf.tile([P, ROUND], F32, name="turns", tag="turns", bufs=1)
+            for i in range(ROUND_CHUNKS):
+                c = r * ROUND_CHUNKS + i
+                cols = slice(i * CHUNK, (i + 1) * CHUNK)
+                u_acc = project(c, W_DT, "gate_dt")
+                nc.scalar.activation(
+                    out=neg_dt[r][:, cols], in_=u_acc[:], func=ACT.Sigmoid, scale=-1.0, bias=neg_b_dt[:, 0:1]
+                )
+                v_acc = project(c, W_PH, "gate_ph")
+                nc.scalar.activation(
+                    out=turns[r][:, cols], in_=v_acc[:], func=ACT.Sigmoid, scale=2.0, bias=two_b_ph[:, 0:1]
+                )
+
+        def step_and_angle(r):
+            nc.scalar.activation(out=neg_dt[r][:], in_=neg_dt[r][:], func=ACT.Ln)
+            decay[r] = sbuf.tile([P, ROUND], F32, name="decay", tag="decay", bufs=1)
+            nc.scalar.activation(out=decay[r][:], in_=neg_dt[r][:], func=ACT.Exp, scale=decay_rate[:, 0:1])
+            nc.vector.scalar_tensor_tensor(
+                out=turns[r][:],
+                in0=neg_dt[r][:],
+                scalar=neg_turn_rate[:, 0:1],
+                in1=turns[r][:],
+                op0=ALU.mult,
+                op1=ALU.add,
+            )
+            sin_d[r] = sbuf.tile([P, ROUND], F32, name="sin_d", tag="sin_d")
+            nc.vector.tensor_scalar_add(out=sin_d[r][:], in0=turns[r][:], scalar1=ROUND_TO_INT)
+            nc.vector.scalar_tensor_tensor(
+                out=sin_d[r][:],
+                in0=sin_d[r][:],
+                scalar=ROUND_TO_INT,
+                in1=turns[r][:],
+                op0=ALU.subtract,
+                op1=ALU.subtract,
+            )
+            cos_d[r] = sbuf.tile([P, ROUND], F32, name="cos_d", tag="cos_d")
+
+        def sine_and_cosine(r, half):
+            cols = slice(half * HALF, (half + 1) * HALF)
+            nc.scalar.activation(out=cos_d[r][:, cols], in_=sin_d[r][:, cols], func=ACT.Sin, scale=math.pi)
+            nc.scalar.activation(out=sin_d[r][:, cols], in_=sin_d[r][:, cols], func=ACT.Sin, scale=TWO_PI)
+            nc.scalar.activation(out=cos_d[r][:, cols], in_=cos_d[r][:, cols], func=ACT.Square, scale=math.sqrt(2.0))
+            nc.vector.tensor_mul(out=sin_d[r][:, cols], in0=sin_d[r][:, cols], in1=decay[r][:, cols])
+            nc.vector.scalar_tensor_tensor(
+                out=cos_d[r][:, cols],
+                in0=cos_d[r][:, cols],
+                scalar=1.0,
+                in1=decay[r][:, cols],
+                op0=ALU.subtract,
+                op1=ALU.mult,
+            )
+
+        def rotate_chunk(c):
+            r, i = divmod(c, ROUND_CHUNKS)
+            cols = slice(i * CHUNK, (i + 1) * CHUNK)
+            cos_t = psum.tile([P, CHUNK], F32, tag="cos_t")
+            sin_t = psum.tile([P, CHUNK], F32, tag="sin_t")
+            for b in range(BLOCKS):
+                rows = slice(i * CHUNK + b * P, i * CHUNK + (b + 1) * P)
+                nc.tensor.transpose(cos_t[:, b * P : (b + 1) * P], cos_d[r][:, rows], identity[:])
+            for b in range(BLOCKS):
+                rows = slice(i * CHUNK + b * P, i * CHUNK + (b + 1) * P)
+                nc.tensor.transpose(sin_t[:, b * P : (b + 1) * P], sin_d[r][:, rows], identity[:])
+            drive = psum.tile([P, CHUNK], F32, tag="drive")
+            for b in range(BLOCKS):
+                for g in range(PASSES):
+                    rows = slice(g * CHUNK + b * P, g * CHUNK + (b + 1) * P)
+                    nc.tensor.matmul_mx(
+                        out=drive[:, b * P : (b + 1) * P],
+                        lhsT=codes[c][:, rows].bitcast(FP8X4),
+                        lhsT_scale=scales[c][:, rows],
+                        rhs=w_words[:, W_B, g, :].bitcast(FP8X4),
+                        rhs_scale=w_scales[:, W_B, g, :],
+                        start=(g == 0),
+                        stop=(g == PASSES - 1),
+                    )
+            by_cos = sbuf.tile([P, 2, CHUNK], F32, tag="by_cos")
+            by_sin = sbuf.tile([P, 2, CHUNK], F32, tag="by_sin")
+            nc.vector.tensor_tensor(
+                out=by_cos[:],
+                in0=state[r][:, :, cols],
+                in1=cos_t[:].unsqueeze(1).to_broadcast([P, 2, CHUNK]),
+                op=ALU.mult,
+            )
+            nc.vector.tensor_tensor(
+                out=by_sin[:],
+                in0=state[r][:, :, cols],
+                in1=sin_t[:].unsqueeze(1).to_broadcast([P, 2, CHUNK]),
+                op=ALU.mult,
+            )
+            nc.vector.tensor_tensor(out=by_cos[:, 0, :], in0=by_cos[:, 0, :], in1=drive[:], op=ALU.add)
+            new_re = sbuf.tile([P, CHUNK], F32, tag="new_re", bufs=3)
+            new_im = sbuf.tile([P, CHUNK], F32, tag="new_im", bufs=3)
+            nc.gpsimd.tensor_tensor(out=new_re[:], in0=by_cos[:, 0, :], in1=by_sin[:, 1, :], op=ALU.subtract)
+            nc.gpsimd.tensor_tensor(out=new_im[:], in0=by_sin[:, 0, :], in1=by_cos[:, 1, :], op=ALU.add)
+            out_cols = slice(c * CHUNK, (c + 1) * CHUNK)
+            nc.sync.dma_start(out=new_re_rows[:, out_cols], in_=new_re[:])
+            nc.sync.dma_start(out=new_im_rows[:, out_cols], in_=new_im[:])
+
+        for k in range(-ROUND_CHUNKS, N_CHUNKS + ROTATE_LAG):
+            ahead = k + ROUND_CHUNKS
+            if ahead + LOADS_AHEAD < N_CHUNKS:
+                load_x(ahead + LOADS_AHEAD)
+            if ahead < N_CHUNKS:
+                transpose_chunk(ahead)
+            if 0 <= ahead - 1 < N_CHUNKS:
+                quantise_chunk(ahead - 1)
+            if k >= ROTATE_LAG:
+                rotate_chunk(k - ROTATE_LAG)
+            if 0 <= k < N_CHUNKS:
+                r, step = divmod(k, ROUND_CHUNKS)
+                if step == 0:
+                    gates(r)
+                elif step == 1:
+                    step_and_angle(r)
+                else:
+                    sine_and_cosine(r, step - 2)

@@ -63,7 +63,6 @@ def tile_mamba3mimoblock_pa_t_kernel(
         consts = stack.enter_context(tc.tile_pool(name="consts", bufs=1))
         sbuf = stack.enter_context(tc.tile_pool(name="sbuf", bufs=2))
         psum = stack.enter_context(tc.psum_pool(name="psum", bufs=1))
-        stack.enter_context(tc.manual_schedule())
 
         x_tiles, grouped, codes, scales = {}, {}, {}, {}
         state, neg_dt, turns, decay, sin_d, cos_d = {}, {}, {}, {}, {}, {}

import math
from contextlib import ExitStack

import concourse.mybir as mybir
from concourse.masks import make_identity

F32 = mybir.dt.float32
BF16 = mybir.dt.bfloat16
I32 = mybir.dt.int32
U32 = mybir.dt.uint32
U8 = mybir.dt.uint8
FP8X4 = mybir.dt.float8_e4m3fn_x4
ACT = mybir.ActivationFunctionType
ALU = mybir.AluOpType

P = 128
ROWS = 8192
D_MODEL = 1024
PASSES = 2
BLOCKS = 4
CHUNK = BLOCKS * P
N_CHUNKS = ROWS // CHUNK
ROWS_PER_PARTITION = ROWS // P
ROUND_CHUNKS = 4
ROUND = ROUND_CHUNKS * CHUNK
HALF = ROUND // 2
N_WEIGHTS = 3
W_DT, W_PH, W_B = 0, 1, 2
LOADS_AHEAD = 2
ROTATE_LAG = 3
ROUND_TO_INT = 1.5 * 2.0**23
TWO_PI = 2.0 * math.pi

FLOPS = 2 * ROWS * D_MODEL * N_WEIGHTS * P


def tile_mamba3mimoblock_pa_t_kernel(
    tc,
    x,
    state_re,
    state_im,
    W_dt_words,
    W_dt_scales,
    b_dt,
    W_ph_words,
    W_ph_scales,
    b_ph,
    W_B_words,
    W_B_scales,
    A_real,
    A_imag,
    out_0,
    out_1,
):
    nc = tc.nc
    x_rows = x.rearrange("(p i) k -> p i k", i=ROWS_PER_PARTITION)
    re_rows = state_re.rearrange("(p i) n -> p (i n)", i=ROWS_PER_PARTITION)
    im_rows = state_im.rearrange("(p i) n -> p (i n)", i=ROWS_PER_PARTITION)
    new_re_rows = out_0.rearrange("(p i) n -> p (i n)", i=ROWS_PER_PARTITION)
    new_im_rows = out_1.rearrange("(p i) n -> p (i n)", i=ROWS_PER_PARTITION)

    with ExitStack() as stack:
        consts = stack.enter_context(tc.tile_pool(name="consts", bufs=1))
        sbuf = stack.enter_context(tc.tile_pool(name="sbuf", bufs=2))
        psum = stack.enter_context(tc.psum_pool(name="psum", bufs=1))

        x_tiles, grouped, codes, scales = {}, {}, {}, {}
        state, neg_dt, turns, decay, sin_d, cos_d = {}, {}, {}, {}, {}, {}

        def load_x(c):
            x_tiles[c] = sbuf.tile([P, BLOCKS, D_MODEL], BF16, name="x_sb", tag="x_sb", bufs=LOADS_AHEAD + 1)
            nc.sync.dma_start(out=x_tiles[c][:], in_=x_rows[:, BLOCKS * c : BLOCKS * (c + 1), :])

        load_x(0)

        w_scales = consts.tile([P, N_WEIGHTS, PASSES, P], U8, align_bytes=64)
        nc.vector.memset(w_scales[:].rearrange("p w g n -> p (w g n)").bitcast(I32), 0)
        w_words = consts.tile([P, N_WEIGHTS, PASSES, P], U32, align_bytes=64)

        def load_weight(w, words, scale_rows):
            for quadrant in range(4):
                nc.sync.dma_start(
                    out=w_scales[32 * quadrant : 32 * quadrant + 4, w, :, :].bitcast(I32),
                    in_=scale_rows[:, 4 * quadrant : 4 * quadrant + 4, :].rearrange("g q n -> q g n").bitcast(I32),
                )
            nc.sync.dma_start(
                out=w_words[:, w, :, :].bitcast(I32),
                in_=words.rearrange("g p n t -> p g (n t)").bitcast(I32),
            )

        load_weight(W_DT, W_dt_words, W_dt_scales)
        load_weight(W_PH, W_ph_words, W_ph_scales)
        load_x(1)
        load_weight(W_B, W_B_words, W_B_scales)

        identity = consts.tile([P, P], F32)
        make_identity(nc, identity[:])
        identity_bf = consts.tile([P, P], BF16)
        make_identity(nc, identity_bf[:])

        vector_rows = consts.tile([P, P], BF16)
        nc.vector.memset(vector_rows[:].bitcast(I32), 0)
        for j, vector in enumerate((b_dt, b_ph, A_real, A_imag)):
            nc.scalar.dma_start(out=vector_rows[j : j + 1, :], in_=vector.unsqueeze(0))
        vector_cols = psum.tile([P, P], BF16, tag="cos_t")
        nc.tensor.transpose(vector_cols[:], vector_rows[:], identity_bf[:])
        per_channel = consts.tile([P, 4], F32)
        nc.vector.tensor_copy(out=per_channel[:], in_=vector_cols[:, 0:4])

        neg_b_dt = consts.tile([P, 1], F32)
        nc.vector.tensor_scalar_mul(out=neg_b_dt[:], in0=per_channel[:, 0:1], scalar1=-1.0)
        two_b_ph = consts.tile([P, 1], F32)
        nc.vector.tensor_scalar_mul(out=two_b_ph[:], in0=per_channel[:, 1:2], scalar1=2.0)
        decay_rate = consts.tile([P, 1], F32)
        nc.scalar.activation(out=decay_rate[:], in_=per_channel[:, 2:3], func=ACT.Exp)
        neg_turn_rate = consts.tile([P, 1], F32)
        nc.vector.tensor_scalar_mul(out=neg_turn_rate[:], in0=per_channel[:, 3:4], scalar1=-1.0 / TWO_PI)

        def transpose_chunk(c):
            grouped[c] = sbuf.tile([P, PASSES, 4 * CHUNK], BF16, name="grouped", tag="grouped", align_bytes=64)
            for g in range(PASSES):
                pairs = grouped[c][:, g, :].bitcast(F32).rearrange("p (row u) -> p row u", u=2)
                for h in range(BLOCKS // 2):
                    xt = psum.tile([P, 2, 2 * P], F32, tag="xt", bufs=3)
                    for u in range(2):
                        for b in range(2):
                            x_words = x_tiles[c][:, 2 * h + b, :].bitcast(F32)
                            nc.tensor.transpose(
                                xt[:, u, P * b : P * (b + 1)],
                                x_words[:, 256 * g + u : 256 * (g + 1) : 2],
                                identity[:],
                            )
                    rows_out = pairs[:, 2 * P * h : 2 * P * (h + 1), :]
                    if h % 2 == 0:
                        nc.scalar.copy(out=rows_out, in_=xt[:].rearrange("p u row -> p row u"))
                    else:
                        nc.vector.tensor_copy(out=rows_out, in_=xt[:].rearrange("p u row -> p row u"))

        def quantise_chunk(c):
            codes[c] = sbuf.tile([P, PASSES * CHUNK], U32, name="codes", tag="codes", bufs=8, align_bytes=64)
            scales[c] = sbuf.tile([P, PASSES * CHUNK], U8, name="scales", tag="scales", bufs=8, align_bytes=64)
            nc.vector.quantize_mx(
                out=codes[c][:].bitcast(FP8X4),
                scales=scales[c][:],
                in_=grouped[c][:].rearrange("p g n -> p (g n)"),
            )

        def project(c, w, tag):
            acc = psum.tile([P, CHUNK], F32, name=tag, tag=tag)
            for g in range(PASSES):
                k_cols = slice(g * CHUNK, (g + 1) * CHUNK)
                nc.tensor.matmul_mx(
                    out=acc[:],
                    lhsT=w_words[:, w, g, :].bitcast(FP8X4),
                    lhsT_scale=w_scales[:, w, g, :],
                    rhs=codes[c][:, k_cols].bitcast(FP8X4),
                    rhs_scale=scales[c][:, k_cols],
                    start=(g == 0),
                    stop=(g == PASSES - 1),
                )
            return acc

        def gates(r):
            state[r] = sbuf.tile([P, 2, ROUND], BF16, name="state", tag="state")
            nc.sync.dma_start(out=state[r][:, 0, :], in_=re_rows[:, r * ROUND : (r + 1) * ROUND])
            nc.sync.dma_start(out=state[r][:, 1, :], in_=im_rows[:, r * ROUND : (r + 1) * ROUND])
            neg_dt[r] = sbuf.tile([P, ROUND], F32, name="neg_dt", tag="neg_dt", bufs=1)
            turns[r] = sbuf.tile([P, ROUND], F32, name="turns", tag="turns", bufs=1)
            for i in range(ROUND_CHUNKS):
                c = r * ROUND_CHUNKS + i
                cols = slice(i * CHUNK, (i + 1) * CHUNK)
                u_acc = project(c, W_DT, "gate_dt")
                nc.scalar.activation(
                    out=neg_dt[r][:, cols], in_=u_acc[:], func=ACT.Sigmoid, scale=-1.0, bias=neg_b_dt[:, 0:1]
                )
                v_acc = project(c, W_PH, "gate_ph")
                nc.scalar.activation(
                    out=turns[r][:, cols], in_=v_acc[:], func=ACT.Sigmoid, scale=2.0, bias=two_b_ph[:, 0:1]
                )

        def step_and_angle(r):
            nc.scalar.activation(out=neg_dt[r][:], in_=neg_dt[r][:], func=ACT.Ln)
            decay[r] = sbuf.tile([P, ROUND], F32, name="decay", tag="decay", bufs=1)
            nc.scalar.activation(out=decay[r][:], in_=neg_dt[r][:], func=ACT.Exp, scale=decay_rate[:, 0:1])
            nc.vector.scalar_tensor_tensor(
                out=turns[r][:],
                in0=neg_dt[r][:],
                scalar=neg_turn_rate[:, 0:1],
                in1=turns[r][:],
                op0=ALU.mult,
                op1=ALU.add,
            )
            sin_d[r] = sbuf.tile([P, ROUND], F32, name="sin_d", tag="sin_d")
            nc.vector.tensor_scalar_add(out=sin_d[r][:], in0=turns[r][:], scalar1=ROUND_TO_INT)
            nc.vector.scalar_tensor_tensor(
                out=sin_d[r][:],
                in0=sin_d[r][:],
                scalar=ROUND_TO_INT,
                in1=turns[r][:],
                op0=ALU.subtract,
                op1=ALU.subtract,
            )
            cos_d[r] = sbuf.tile([P, ROUND], F32, name="cos_d", tag="cos_d")

        def sine_and_cosine(r, half):
            cols = slice(half * HALF, (half + 1) * HALF)
            nc.scalar.activation(out=cos_d[r][:, cols], in_=sin_d[r][:, cols], func=ACT.Sin, scale=math.pi)
            nc.scalar.activation(out=sin_d[r][:, cols], in_=sin_d[r][:, cols], func=ACT.Sin, scale=TWO_PI)
            nc.scalar.activation(out=cos_d[r][:, cols], in_=cos_d[r][:, cols], func=ACT.Square, scale=math.sqrt(2.0))
            nc.vector.tensor_mul(out=sin_d[r][:, cols], in0=sin_d[r][:, cols], in1=decay[r][:, cols])
            nc.vector.scalar_tensor_tensor(
                out=cos_d[r][:, cols],
                in0=cos_d[r][:, cols],
                scalar=1.0,
                in1=decay[r][:, cols],
                op0=ALU.subtract,
                op1=ALU.mult,
            )

        def rotate_chunk(c):
            r, i = divmod(c, ROUND_CHUNKS)
            cols = slice(i * CHUNK, (i + 1) * CHUNK)
            cos_t = psum.tile([P, CHUNK], F32, tag="cos_t")
            sin_t = psum.tile([P, CHUNK], F32, tag="sin_t")
            for b in range(BLOCKS):
                rows = slice(i * CHUNK + b * P, i * CHUNK + (b + 1) * P)
                nc.tensor.transpose(cos_t[:, b * P : (b + 1) * P], cos_d[r][:, rows], identity[:])
            for b in range(BLOCKS):
                rows = slice(i * CHUNK + b * P, i * CHUNK + (b + 1) * P)
                nc.tensor.transpose(sin_t[:, b * P : (b + 1) * P], sin_d[r][:, rows], identity[:])
            drive = psum.tile([P, CHUNK], F32, tag="drive")
            for b in range(BLOCKS):
                for g in range(PASSES):
                    rows = slice(g * CHUNK + b * P, g * CHUNK + (b + 1) * P)
                    nc.tensor.matmul_mx(
                        out=drive[:, b * P : (b + 1) * P],
                        lhsT=codes[c][:, rows].bitcast(FP8X4),
                        lhsT_scale=scales[c][:, rows],
                        rhs=w_words[:, W_B, g, :].bitcast(FP8X4),
                        rhs_scale=w_scales[:, W_B, g, :],
                        start=(g == 0),
                        stop=(g == PASSES - 1),
                    )
            by_cos = sbuf.tile([P, 2, CHUNK], F32, tag="by_cos")
            by_sin = sbuf.tile([P, 2, CHUNK], F32, tag="by_sin")
            nc.vector.tensor_tensor(
                out=by_cos[:],
                in0=state[r][:, :, cols],
                in1=cos_t[:].unsqueeze(1).to_broadcast([P, 2, CHUNK]),
                op=ALU.mult,
            )
            nc.vector.tensor_tensor(
                out=by_sin[:],
                in0=state[r][:, :, cols],
                in1=sin_t[:].unsqueeze(1).to_broadcast([P, 2, CHUNK]),
                op=ALU.mult,
            )
            nc.vector.tensor_tensor(out=by_cos[:, 0, :], in0=by_cos[:, 0, :], in1=drive[:], op=ALU.add)
            new_re = sbuf.tile([P, CHUNK], F32, tag="new_re", bufs=3)
            new_im = sbuf.tile([P, CHUNK], F32, tag="new_im", bufs=3)
            nc.gpsimd.tensor_tensor(out=new_re[:], in0=by_cos[:, 0, :], in1=by_sin[:, 1, :], op=ALU.subtract)
            nc.gpsimd.tensor_tensor(out=new_im[:], in0=by_sin[:, 0, :], in1=by_cos[:, 1, :], op=ALU.add)
            out_cols = slice(c * CHUNK, (c + 1) * CHUNK)
            nc.sync.dma_start(out=new_re_rows[:, out_cols], in_=new_re[:])
            nc.sync.dma_start(out=new_im_rows[:, out_cols], in_=new_im[:])

        for k in range(-ROUND_CHUNKS, N_CHUNKS + ROTATE_LAG):
            ahead = k + ROUND_CHUNKS
            if ahead + LOADS_AHEAD < N_CHUNKS:
                load_x(ahead + LOADS_AHEAD)
            if ahead < N_CHUNKS:
                transpose_chunk(ahead)
            if 0 <= ahead - 1 < N_CHUNKS:
                quantise_chunk(ahead - 1)
            if k >= ROTATE_LAG:
                rotate_chunk(k - ROTATE_LAG)
            if 0 <= k < N_CHUNKS:
                r, step = divmod(k, ROUND_CHUNKS)
                if step == 0:
                    gates(r)
                elif step == 1:
                    step_and_angle(r)
                else:
                    sine_and_cosine(r, step - 2)
